import numpy as np
import ml_dtypes


def mxq(x, axis, fmt="e4m3"):
    dtype, down = {"e4m3": (ml_dtypes.float8_e4m3fn, 7), "e5m2": (ml_dtypes.float8_e5m2, 14)}[fmt]
    v = np.moveaxis(np.asarray(x, np.float32).astype(ml_dtypes.bfloat16).astype(np.float64), axis, -1)
    blocks = v.reshape(v.shape[:-1] + (-1, 32))
    amax = np.abs(blocks).max(-1, keepdims=True)
    byte = np.maximum(np.where(amax > 0, np.frexp(amax)[1] - 1 + 127, 0) - down, 1)
    scale = np.exp2(byte - 127.0)
    codes = (blocks / scale).astype(np.float32).astype(dtype).astype(np.float64)
    return np.moveaxis((codes * scale).reshape(v.shape), -1, axis)


WIDE = False


def mx_kscale(k):
    if not WIDE:
        return np.ones(k)
    levels = np.array([10, -10, 5, -5, 0])
    a = np.random.permutation(np.resize(levels, k // 512 * 4)).reshape(k // 512, 4)
    idx = np.arange(k)
    return np.exp2(a[idx // 512, idx % 128 // 32])


BF16 = ml_dtypes.bfloat16


def bf(x):
    return np.asarray(x, np.float32).astype(BF16)


def f64(x):
    return np.asarray(x).astype(np.float64)


B, F, D = 256, 128, 24
K = F * D
LN_EPS = 1e-5


def layernorm(x, w, b):
    mu = x.mean(-1, keepdims=True)
    var = ((x - mu) ** 2).mean(-1, keepdims=True)
    return (x - mu) / np.sqrt(var + LN_EPS) * w + b


def setup_inputs():
    s = mx_kscale(K)
    sf = s.reshape(F, D)
    a = np.random.standard_normal((B, F, D))
    c = np.random.standard_normal((B, F, D))
    return {"r": bf(np.random.standard_normal((B, F, D)) * sf),
            "p": bf(np.random.standard_normal((B, F, D)) * sf),
            "log_lam": bf(0.5 * np.log(a ** 2 + c ** 2 + 1e-8)),
            "theta": bf(np.random.uniform(-np.pi, np.pi, (B, F, D))),
            "inter_orders": bf(np.random.standard_normal((F, F)) / np.sqrt(F)),
            "im_w": bf(np.random.standard_normal((K, K)) / np.sqrt(K) / s[:, None]),
            "im_b": bf(np.random.standard_normal(K) * 0.3),
            "bias_lam": bf(np.random.standard_normal((1, D, F)) * 0.3),
            "bias_theta": bf(np.random.standard_normal((1, D, F)) * 0.3),
            "norm_r_w": bf(1.0 + 0.2 * np.random.standard_normal(D)),
            "norm_r_b": bf(0.2 * np.random.standard_normal(D)),
            "norm_p_w": bf(1.0 + 0.2 * np.random.standard_normal(D)),
            "norm_p_b": bf(0.2 * np.random.standard_normal(D))}


def reference(r, p, log_lam, theta, inter_orders, im_w, im_b, bias_lam, bias_theta, norm_r_w, norm_r_b, norm_p_w, norm_p_b):
    io = f64(inter_orders)
    lam_t = np.swapaxes(f64(log_lam), -2, -1) @ io + f64(bias_lam)
    theta_t = np.swapaxes(f64(theta), -2, -1) @ io + f64(bias_theta)
    lam = np.swapaxes(np.exp(lam_t), -2, -1)
    th = np.swapaxes(theta_t, -2, -1)
    wq = mxq(f64(im_w), 0, "e4m3")
    r_lin = np.maximum((mxq(f64(r).reshape(B, K), 1, "e4m3") @ wq) + f64(im_b), 0.0).reshape(B, F, D)
    p_lin = np.maximum((mxq(f64(p).reshape(B, K), 1, "e4m3") @ wq) + f64(im_b), 0.0).reshape(B, F, D)
    o_r = r_lin + lam * np.cos(th)
    o_p = p_lin + lam * np.sin(th)
    return (layernorm(o_r, f64(norm_r_w), f64(norm_r_b)), layernorm(o_p, f64(norm_p_w), f64(norm_p_b)))

@@ -1,0 +1,318 @@
+import math
+
+import concourse.mybir as mybir
+from concourse.masks import make_identity
+
+F32 = mybir.dt.float32
+BF16 = mybir.dt.bfloat16
+U32 = mybir.dt.uint32
+U8 = mybir.dt.uint8
+FP8X4 = mybir.dt.float8_e4m3fn_x4
+ACT = mybir.ActivationFunctionType
+ALU = mybir.AluOpType
+AXIS_X = mybir.AxisListType.X
+
+P = 128
+BATCH = 256
+FIELDS = 128
+EMB = 24
+K = FIELDS * EMB
+B_TILES = BATCH // P
+M_TILES = 2 * B_TILES
+K_PASS = 512
+PASSES = K // K_PASS
+HALF = K_PASS // 2
+ROUND_FIELDS = 16
+ROUND_COLS = ROUND_FIELDS * EMB
+ROUNDS = FIELDS // ROUND_FIELDS
+WIDE = 256
+QUAD = 4
+LN_EPS = 1e-5
+ROUNDS_AHEAD = 4
+VECTOR_ROUNDS = 4
+ROUND_MAGIC = 12582912.0
+
+FLOPS = 2 * (2 * BATCH) * K * K + 2 * 2 * BATCH * EMB * FIELDS * FIELDS
+
+
+def tile_eulerinteractionlayer_pa_kernel(
+    tc,
+    r,
+    p,
+    log_lam,
+    theta,
+    inter_orders,
+    im_w,
+    im_b,
+    bias_lam,
+    bias_theta,
+    norm_r_w,
+    norm_r_b,
+    norm_p_w,
+    norm_p_b,
+    out_0,
+    out_1,
+):
+    nc = tc.nc
+    with (
+        tc.tile_pool(name="keep", bufs=1) as keep,
+        tc.tile_pool(name="w_raw", bufs=8) as w_raw_pool,
+        tc.tile_pool(name="w_grouped", bufs=PASSES) as w_grouped_pool,
+        tc.tile_pool(name="w_mx", bufs=ROUNDS_AHEAD * PASSES) as w_mx_pool,
+        tc.psum_pool(name="acc", bufs=M_TILES) as acc_pool,
+        tc.psum_pool(name="aux", bufs=4) as aux_pool,
+    ):
+        ident_f32 = keep.tile([P, P], F32)
+        make_identity(nc, ident_f32[:])
+        ident_bf = keep.tile([P, P], BF16)
+        make_identity(nc, ident_bf[:])
+        ones_bf = keep.tile([P, P], BF16)
+        nc.vector.memset(ones_bf[:], 1.0)
+        eps = keep.tile([P, 1], F32)
+        nc.vector.memset(eps[:], LN_EPS)
+        orders = keep.tile([P, FIELDS], BF16)
+        nc.sync.dma_start(out=orders[:], in_=inter_orders)
+
+        a_codes = keep.tile([P, M_TILES, PASSES, P], U32, align_bytes=64)
+        a_scales = keep.tile([P, M_TILES, PASSES, P], U8, align_bytes=64)
+        neg_polar = keep.tile([P, M_TILES, K], F32)
+        imb_all = keep.tile([P, K], BF16)
+        ln_gain = keep.tile([P, M_TILES, EMB], F32)
+        ln_bias = keep.tile([P, M_TILES, EMB], F32)
+
+        with tc.tile_pool(name="head", bufs=1) as head:
+            for m in range(M_TILES):
+                source = r if m < B_TILES else p
+                rows = slice((m % B_TILES) * P, (m % B_TILES + 1) * P)
+                raw = head.tile([P, K], BF16, tag="raw", bufs=3)
+                nc.sync.dma_start(out=raw[:], in_=source.rearrange("b f d -> b (f d)")[rows, :])
+                raw_words = raw[:].bitcast(F32)
+                a_grouped = head.tile([P, PASSES, P, 4], BF16, align_bytes=64)
+                a_grouped_words = a_grouped[:].bitcast(F32)
+                for c0 in range(0, PASSES, 2):
+                    flipped = aux_pool.tile([P, 2, 2, P], F32, tag="aux")
+                    for j in range(2):
+                        for u in range(2):
+                            first = ((c0 + j) * K_PASS + u * HALF) // 2
+                            nc.tensor.transpose(
+                                flipped[:, j, u, :], raw_words[:, first : first + P], ident_f32[:]
+                            )
+                    nc.vector.tensor_copy(
+                        out=a_grouped_words[:, c0 : c0 + 2, :, :],
+                        in_=flipped[:].rearrange("q j u b -> q j b u"),
+                    )
+                for lo, hi in ((0, 4), (4, 6)):
+                    nc.vector.quantize_mx(
+                        out=a_codes[:, m, lo:hi, :].rearrange("q c b -> q (c b)").bitcast(FP8X4),
+                        scales=a_scales[:, m, lo:hi, :].rearrange("q c b -> q (c b)"),
+                        in_=a_grouped[:, lo:hi, :, :].rearrange("q c b t -> q (c b t)"),
+                    )
+
+            nc.sync.dma_start(out=imb_all[:], in_=im_b.partition_broadcast(P))
+            for vec, dest, first in (
+                (norm_r_w, ln_gain, 0),
+                (norm_p_w, ln_gain, B_TILES),
+                (norm_r_b, ln_bias, 0),
+                (norm_p_b, ln_bias, B_TILES),
+            ):
+                spread = head.tile([P, EMB], BF16, tag="spread", bufs=4)
+                nc.sync.dma_start(out=spread[:], in_=vec.partition_broadcast(P))
+                nc.vector.tensor_copy(
+                    out=dest[:, first : first + B_TILES, :],
+                    in_=spread[:].unsqueeze(1).to_broadcast([P, B_TILES, EMB]),
+                )
+
+            for kind, x, bias in (("lam", log_lam, bias_lam), ("theta", theta, bias_theta)):
+                bias_row = head.tile([P, K], BF16, tag="bias_row", bufs=2)
+                nc.gpsimd.memset(bias_row[:], 0.0)
+                nc.sync.dma_start(out=bias_row[0:1, :], in_=bias.rearrange("o d g -> o (d g)"))
+                for bt in range(B_TILES):
+                    raw = head.tile([P, K], BF16, tag="raw", bufs=3)
+                    nc.sync.dma_start(
+                        out=raw[:],
+                        in_=x.rearrange("b f d -> b (f d)")[bt * P : (bt + 1) * P, :],
+                    )
+                    by_emb = raw[:].rearrange("b (f d) -> b f d", d=EMB)
+                    x_t = head.tile([P, EMB, P], BF16, tag="x_t", bufs=2)
+                    for d0 in range(0, EMB, QUAD):
+                        flipped = aux_pool.tile([P, QUAD, P], BF16, tag="aux")
+                        for i in range(QUAD):
+                            nc.tensor.transpose(flipped[:, i, :], by_emb[:, :, d0 + i], ident_bf[:])
+                        nc.scalar.copy(out=x_t[:, d0 : d0 + QUAD, :], in_=flipped[:])
+                    for d0 in range(0, EMB, QUAD):
+                        mixed = aux_pool.tile([P, QUAD, FIELDS], F32, tag="aux")
+                        for i in range(QUAD):
+                            d = d0 + i
+                            nc.tensor.matmul(
+                                mixed[:, i, :],
+                                lhsT=ones_bf[:],
+                                rhs=bias_row[:, d * FIELDS : (d + 1) * FIELDS],
+                                start=True,
+                                stop=False,
+                            )
+                            nc.tensor.matmul(
+                                mixed[:, i, :],
+                                lhsT=x_t[:, d, :],
+                                rhs=orders[:],
+                                start=False,
+                                stop=True,
+                            )
+                        by_field = mixed[:].rearrange("b i g -> b g i")
+                        if kind == "lam":
+                            nc.scalar.activation(
+                                out=neg_polar[:, bt, :].rearrange("b (g d) -> b g d", d=EMB)[
+                                    :, :, d0 : d0 + QUAD
+                                ],
+                                in_=by_field,
+                                func=ACT.Exp,
+                            )
+                        else:
+                            nc.scalar.activation(
+                                out=neg_polar[:, B_TILES + bt, :].rearrange(
+                                    "b (g d) -> b g d", d=EMB
+                                )[:, :, d0 : d0 + QUAD],
+                                in_=by_field,
+                                func=ACT.Copy,
+                                scale=1.0 / (2.0 * math.pi),
+                            )
+            for bt in range(B_TILES):
+                lam = neg_polar[:, bt, :]
+                turns = neg_polar[:, B_TILES + bt, :]
+                part = head.tile([P, K], F32, bufs=2)
+                nc.vector.tensor_scalar(
+                    out=part[:],
+                    in0=turns,
+                    scalar1=ROUND_MAGIC,
+                    scalar2=ROUND_MAGIC,
+                    op0=ALU.add,
+                    op1=ALU.subtract,
+                )
+                nc.vector.tensor_tensor(out=part[:], in0=part[:], in1=turns, op=ALU.subtract)
+                nc.scalar.activation(
+                    out=neg_polar[:, B_TILES + bt, :], in_=part[:], func=ACT.Sin, scale=2.0 * math.pi
+                )
+                half_sin = part
+                nc.scalar.activation(out=half_sin[:], in_=part[:], func=ACT.Sin, scale=math.pi)
+                nc.scalar.activation(
+                    out=half_sin[:], in_=half_sin[:], func=ACT.Square, scale=math.sqrt(2.0)
+                )
+                nc.vector.tensor_tensor(
+                    out=neg_polar[:, B_TILES + bt, :],
+                    in0=neg_polar[:, B_TILES + bt, :],
+                    in1=lam,
+                    op=ALU.mult,
+                )
+                nc.vector.scalar_tensor_tensor(
+                    out=lam, in0=half_sin[:], scalar=1.0, in1=lam, op0=ALU.subtract, op1=ALU.mult
+                )
+
+        with tc.tile_pool(name="tail", bufs=2) as tail:
+            for rnd in range(ROUNDS):
+                cols = slice(rnd * ROUND_COLS, (rnd + 1) * ROUND_COLS)
+                w_codes = []
+                w_scales = []
+                for c in range(PASSES):
+                    w_raw = w_raw_pool.tile([P, 4, ROUND_COLS], BF16)
+                    for u in range(2):
+                        first = c * K_PASS + u * HALF
+                        nc.sync.dma_start(
+                            out=w_raw[:, 2 * u : 2 * u + 2, :],
+                            in_=im_w[first : first + HALF, cols].rearrange("(q e) n -> q e n", e=2),
+                        )
+                    w_grouped = w_grouped_pool.tile([P, ROUND_COLS, 4], BF16, align_bytes=64)
+                    if rnd < VECTOR_ROUNDS:
+                        nc.vector.tensor_copy(
+                            out=w_grouped[:].rearrange("q (n i) t -> q n t i", i=4),
+                            in_=w_raw[:].rearrange("q t (n i) -> q n t i", i=4),
+                        )
+                    else:
+                        nc.scalar.copy(
+                            out=w_grouped[:].rearrange("q (n i) t -> q n t i", i=4),
+                            in_=w_raw[:].rearrange("q t (n i) -> q n t i", i=4),
+                        )
+                    codes = w_mx_pool.tile([P, ROUND_COLS], U32, align_bytes=64, name="codes")
+                    scales = w_mx_pool.tile([P, ROUND_COLS], U8, align_bytes=64, name="scales")
+                    for lo, hi in ((0, WIDE), (WIDE, ROUND_COLS)):
+                        nc.vector.quantize_mx(
+                            out=codes[:, lo:hi].bitcast(FP8X4),
+                            scales=scales[:, lo:hi],
+                            in_=w_grouped[:, lo:hi, :].rearrange("q n t -> q (n t)"),
+                        )
+                    w_codes.append(codes)
+                    w_scales.append(scales)
+
+                biased = tail.tile([P, M_TILES, ROUND_COLS], F32)
+                for m in range(M_TILES):
+                    acc = acc_pool.tile([P, ROUND_COLS], F32)
+                    for lo, hi in ((0, WIDE), (WIDE, ROUND_COLS)):
+                        for c in range(PASSES):
+                            nc.tensor.matmul_mx(
+                                out=acc[:, lo:hi],
+                                lhsT=a_codes[:, m, c, :].bitcast(FP8X4),
+                                lhsT_scale=a_scales[:, m, c, :],
+                                rhs=w_codes[c][:, lo:hi].bitcast(FP8X4),
+                                rhs_scale=w_scales[c][:, lo:hi],
+                                start=(c == 0),
+                                stop=(c == PASSES - 1),
+                            )
+                    nc.vector.tensor_tensor(
+                        out=biased[:, m, :], in0=acc[:], in1=imb_all[:, cols], op=ALU.add
+                    )
+                groups = M_TILES * ROUND_FIELDS
+                o = tail.tile([P, M_TILES, ROUND_COLS], F32)
+                nc.vector.scalar_tensor_tensor(
+                    out=o[:],
+                    in0=biased[:],
+                    scalar=0.0,
+                    in1=neg_polar[:, :, cols],
+                    op0=ALU.max,
+                    op1=ALU.subtract,
+                )
+                o_groups = o[:].rearrange("b m (g d) -> b (m g) d", d=EMB)
+                total = tail.tile([P, groups], F32)
+                nc.vector.tensor_reduce(out=total[:], in_=o_groups, axis=AXIS_X, op=ALU.add)
+                neg_mean = tail.tile([P, groups], F32)
+                nc.vector.tensor_scalar(
+                    out=neg_mean[:], in0=total[:], scalar1=-1.0 / EMB, scalar2=None, op0=ALU.mult
+                )
+                squares = tail.tile([P, groups, EMB], F32)
+                spread2 = tail.tile([P, groups], F32)
+                for j in range(groups):
+                    nc.scalar.activation(
+                        out=squares[:, j, :],
+                        in_=o_groups[:, j, :],
+                        func=ACT.Square,
+                        bias=neg_mean[:, j : j + 1],
+                        accum_out=spread2[:, j : j + 1],
+                    )
+                std = tail.tile([P, groups], F32)
+                nc.scalar.activation(
+                    out=std[:], in_=spread2[:], func=ACT.Sqrt, scale=1.0 / EMB, bias=eps[:, 0:1]
+                )
+                rstd = tail.tile([P, groups], F32)
+                nc.vector.reciprocal(out=rstd[:], in_=std[:])
+                shift = tail.tile([P, groups], F32)
+                nc.vector.tensor_tensor(out=shift[:], in0=neg_mean[:], in1=rstd[:], op=ALU.mult)
+                centred = tail.tile([P, groups, EMB], F32)
+                for j in range(groups):
+                    nc.scalar.activation(
+                        out=centred[:, j, :],
+                        in_=o_groups[:, j, :],
+                        func=ACT.Identity,
+                        scale=rstd[:, j : j + 1],
+                        bias=shift[:, j : j + 1],
+                    )
+                by_tile = centred[:].rearrange("b (m g) d -> b m g d", m=M_TILES)
+                full = [P, M_TILES, ROUND_FIELDS, EMB]
+                nc.vector.tensor_tensor(
+                    out=by_tile, in0=by_tile, in1=ln_gain[:].unsqueeze(2).to_broadcast(full), op=ALU.mult
+                )
+                y = tail.tile([P, M_TILES, ROUND_FIELDS, EMB], F32)
+                nc.vector.tensor_tensor(
+                    out=y[:], in0=by_tile, in1=ln_bias[:].unsqueeze(2).to_broadcast(full), op=ALU.add
+                )
+                for dest, first in ((out_0, 0), (out_1, B_TILES)):
+                    nc.gpsimd.dma_start(
+                        out=dest.rearrange("(t b) f d -> b t (f d)", t=B_TILES)[:, :, cols],
+                        in_=y[:, first : first + B_TILES, :, :].rearrange("b t g d -> b t (g d)"),
+                    )

@@ -29,7 +29,7 @@ WIDE = 256
 QUAD = 4
 LN_EPS = 1e-5
 ROUNDS_AHEAD = 4
-VECTOR_ROUNDS = 4
+VECTOR_ROUNDS = 3
 ROUND_MAGIC = 12582912.0
 
 FLOPS = 2 * (2 * BATCH) * K * K + 2 * 2 * BATCH * EMB * FIELDS * FIELDS
@@ -97,7 +97,7 @@ def tile_eulerinteractionlayer_pa_kernel(
                             nc.tensor.transpose(
                                 flipped[:, j, u, :], raw_words[:, first : first + P], ident_f32[:]
                             )
-                    nc.vector.tensor_copy(
+                    nc.scalar.copy(
                         out=a_grouped_words[:, c0 : c0 + 2, :, :],
                         in_=flipped[:].rearrange("q j u b -> q j b u"),
                     )
@@ -271,44 +271,40 @@ def tile_eulerinteractionlayer_pa_kernel(
                 o_groups = o[:].rearrange("b m (g d) -> b (m g) d", d=EMB)
                 total = tail.tile([P, groups], F32)
                 nc.vector.tensor_reduce(out=total[:], in_=o_groups, axis=AXIS_X, op=ALU.add)
-                neg_mean = tail.tile([P, groups], F32)
-                nc.vector.tensor_scalar(
-                    out=neg_mean[:], in0=total[:], scalar1=-1.0 / EMB, scalar2=None, op0=ALU.mult
+                centred = tail.tile([P, groups, EMB], F32)
+                nc.vector.scalar_tensor_tensor(
+                    out=centred[:],
+                    in0=total[:].unsqueeze(2).to_broadcast([P, groups, EMB]),
+                    scalar=-1.0 / EMB,
+                    in1=o_groups,
+                    op0=ALU.mult,
+                    op1=ALU.add,
                 )
                 squares = tail.tile([P, groups, EMB], F32)
+                nc.scalar.activation(out=squares[:], in_=centred[:], func=ACT.Square)
                 spread2 = tail.tile([P, groups], F32)
-                for j in range(groups):
-                    nc.scalar.activation(
-                        out=squares[:, j, :],
-                        in_=o_groups[:, j, :],
-                        func=ACT.Square,
-                        bias=neg_mean[:, j : j + 1],
-                        accum_out=spread2[:, j : j + 1],
-                    )
-                std = tail.tile([P, groups], F32)
-                nc.scalar.activation(
-                    out=std[:], in_=spread2[:], func=ACT.Sqrt, scale=1.0 / EMB, bias=eps[:, 0:1]
-                )
+                nc.vector.tensor_reduce(out=spread2[:], in_=squares[:], axis=AXIS_X, op=ALU.add)
                 rstd = tail.tile([P, groups], F32)
-                nc.vector.reciprocal(out=rstd[:], in_=std[:])
-                shift = tail.tile([P, groups], F32)
-                nc.vector.tensor_tensor(out=shift[:], in0=neg_mean[:], in1=rstd[:], op=ALU.mult)
-                centred = tail.tile([P, groups, EMB], F32)
-                for j in range(groups):
-                    nc.scalar.activation(
-                        out=centred[:, j, :],
-                        in_=o_groups[:, j, :],
-                        func=ACT.Identity,
-                        scale=rstd[:, j : j + 1],
-                        bias=shift[:, j : j + 1],
-                    )
+                nc.scalar.activation(
+                    out=rstd[:],
+                    in_=spread2[:],
+                    func=ACT.Abs_reciprocal_sqrt,
+                    scale=1.0 / EMB,
+                    bias=eps[:, 0:1],
+                )
+                nc.vector.tensor_tensor(
+                    out=centred[:],
+                    in0=centred[:],
+                    in1=rstd[:].unsqueeze(2).to_broadcast([P, groups, EMB]),
+                    op=ALU.mult,
+                )
                 by_tile = centred[:].rearrange("b (m g) d -> b m g d", m=M_TILES)
                 full = [P, M_TILES, ROUND_FIELDS, EMB]
-                nc.vector.tensor_tensor(
+                nc.gpsimd.tensor_tensor(
                     out=by_tile, in0=by_tile, in1=ln_gain[:].unsqueeze(2).to_broadcast(full), op=ALU.mult
                 )
                 y = tail.tile([P, M_TILES, ROUND_FIELDS, EMB], F32)
-                nc.vector.tensor_tensor(
+                nc.gpsimd.tensor_tensor(
                     out=y[:], in0=by_tile, in1=ln_bias[:].unsqueeze(2).to_broadcast(full), op=ALU.add
                 )
                 for dest, first in ((out_0, 0), (out_1, B_TILES)):

@@ -29,7 +29,7 @@ WIDE = 256
 QUAD = 4
 LN_EPS = 1e-5
 ROUNDS_AHEAD = 4
-VECTOR_ROUNDS = 3
+VECTOR_ROUNDS = 4
 ROUND_MAGIC = 12582912.0
 
 FLOPS = 2 * (2 * BATCH) * K * K + 2 * 2 * BATCH * EMB * FIELDS * FIELDS
@@ -97,7 +97,7 @@ def tile_eulerinteractionlayer_pa_kernel(
                             nc.tensor.transpose(
                                 flipped[:, j, u, :], raw_words[:, first : first + P], ident_f32[:]
                             )
-                    nc.scalar.copy(
+                    nc.vector.tensor_copy(
                         out=a_grouped_words[:, c0 : c0 + 2, :, :],
                         in_=flipped[:].rearrange("q j u b -> q j b u"),
                     )
@@ -284,14 +284,12 @@ def tile_eulerinteractionlayer_pa_kernel(
                 nc.scalar.activation(out=squares[:], in_=centred[:], func=ACT.Square)
                 spread2 = tail.tile([P, groups], F32)
                 nc.vector.tensor_reduce(out=spread2[:], in_=squares[:], axis=AXIS_X, op=ALU.add)
-                rstd = tail.tile([P, groups], F32)
+                std = tail.tile([P, groups], F32)
                 nc.scalar.activation(
-                    out=rstd[:],
-                    in_=spread2[:],
-                    func=ACT.Abs_reciprocal_sqrt,
-                    scale=1.0 / EMB,
-                    bias=eps[:, 0:1],
+                    out=std[:], in_=spread2[:], func=ACT.Sqrt, scale=1.0 / EMB, bias=eps[:, 0:1]
                 )
+                rstd = tail.tile([P, groups], F32)
+                nc.vector.reciprocal(out=rstd[:], in_=std[:])
                 nc.vector.tensor_tensor(
                     out=centred[:],
                     in0=centred[:],
@@ -300,11 +298,11 @@ def tile_eulerinteractionlayer_pa_kernel(
                 )
                 by_tile = centred[:].rearrange("b (m g) d -> b m g d", m=M_TILES)
                 full = [P, M_TILES, ROUND_FIELDS, EMB]
-                nc.gpsimd.tensor_tensor(
+                nc.vector.tensor_tensor(
                     out=by_tile, in0=by_tile, in1=ln_gain[:].unsqueeze(2).to_broadcast(full), op=ALU.mult
                 )
                 y = tail.tile([P, M_TILES, ROUND_FIELDS, EMB], F32)
-                nc.gpsimd.tensor_tensor(
+                nc.vector.tensor_tensor(
                     out=y[:], in0=by_tile, in1=ln_bias[:].unsqueeze(2).to_broadcast(full), op=ALU.add
                 )
                 for dest, first in ((out_0, 0), (out_1, B_TILES)):

@@ -29,7 +29,7 @@ WIDE = 256
 QUAD = 4
 LN_EPS = 1e-5
 ROUNDS_AHEAD = 4
-VECTOR_ROUNDS = 4
+VECTOR_ROUNDS = 3
 ROUND_MAGIC = 12582912.0
 
 FLOPS = 2 * (2 * BATCH) * K * K + 2 * 2 * BATCH * EMB * FIELDS * FIELDS
@@ -64,8 +64,6 @@ def tile_eulerinteractionlayer_pa_kernel(
     ):
         ident_f32 = keep.tile([P, P], F32)
         make_identity(nc, ident_f32[:])
-        ident_bf = keep.tile([P, P], BF16)
-        make_identity(nc, ident_bf[:])
         ones_bf = keep.tile([P, P], BF16)
         nc.vector.memset(ones_bf[:], 1.0)
         eps = keep.tile([P, 1], F32)
@@ -97,7 +95,7 @@ def tile_eulerinteractionlayer_pa_kernel(
                             nc.tensor.transpose(
                                 flipped[:, j, u, :], raw_words[:, first : first + P], ident_f32[:]
                             )
-                    nc.vector.tensor_copy(
+                    nc.scalar.copy(
                         out=a_grouped_words[:, c0 : c0 + 2, :, :],
                         in_=flipped[:].rearrange("q j u b -> q j b u"),
                     )
@@ -122,8 +120,8 @@ def tile_eulerinteractionlayer_pa_kernel(
                     in_=spread[:].unsqueeze(1).to_broadcast([P, B_TILES, EMB]),
                 )
 
-            for kind, x, bias in (("lam", log_lam, bias_lam), ("theta", theta, bias_theta)):
-                bias_row = head.tile([P, K], BF16, tag="bias_row", bufs=2)
+            for kind, x, bias in (("theta", theta, bias_theta), ("lam", log_lam, bias_lam)):
+                bias_row = head.tile([P, K], BF16, tag="bias_row", bufs=1)
                 nc.gpsimd.memset(bias_row[:], 0.0)
                 nc.sync.dma_start(out=bias_row[0:1, :], in_=bias.rearrange("o d g -> o (d g)"))
                 for bt in range(B_TILES):
@@ -132,13 +130,20 @@ def tile_eulerinteractionlayer_pa_kernel(
                         out=raw[:],
                         in_=x.rearrange("b f d -> b (f d)")[bt * P : (bt + 1) * P, :],
                     )
-                    by_emb = raw[:].rearrange("b (f d) -> b f d", d=EMB)
-                    x_t = head.tile([P, EMB, P], BF16, tag="x_t", bufs=2)
-                    for d0 in range(0, EMB, QUAD):
-                        flipped = aux_pool.tile([P, QUAD, P], BF16, tag="aux")
+                    by_word = head.tile([P, EMB // 2, FIELDS], F32, tag="by_word", bufs=1)
+                    nc.vector.tensor_copy(
+                        out=by_word[:],
+                        in_=raw[:].bitcast(F32).rearrange("b (f w) -> b w f", w=EMB // 2),
+                    )
+                    x_t = head.tile([P, EMB // 2, P, 2], BF16, tag="x_t", bufs=2)
+                    x_t_words = x_t[:].bitcast(F32)
+                    for w0 in range(0, EMB // 2, QUAD):
+                        flipped = aux_pool.tile([P, QUAD, P], F32, tag="aux")
                         for i in range(QUAD):
-                            nc.tensor.transpose(flipped[:, i, :], by_emb[:, :, d0 + i], ident_bf[:])
-                        nc.scalar.copy(out=x_t[:, d0 : d0 + QUAD, :], in_=flipped[:])
+                            nc.tensor.transpose(flipped[:, i, :], by_word[:, w0 + i, :], ident_f32[:])
+                        nc.scalar.copy(
+                            out=x_t_words[:, w0 : w0 + QUAD, :, 0], in_=flipped[:]
+                        )
                     for d0 in range(0, EMB, QUAD):
                         mixed = aux_pool.tile([P, QUAD, FIELDS], F32, tag="aux")
                         for i in range(QUAD):
@@ -152,7 +157,7 @@ def tile_eulerinteractionlayer_pa_kernel(
                             )
                             nc.tensor.matmul(
                                 mixed[:, i, :],
-                                lhsT=x_t[:, d, :],
+                                lhsT=x_t[:, d // 2, :, d % 2],
                                 rhs=orders[:],
                                 start=False,
                                 stop=True,
@@ -284,12 +289,14 @@ def tile_eulerinteractionlayer_pa_kernel(
                 nc.scalar.activation(out=squares[:], in_=centred[:], func=ACT.Square)
                 spread2 = tail.tile([P, groups], F32)
                 nc.vector.tensor_reduce(out=spread2[:], in_=squares[:], axis=AXIS_X, op=ALU.add)
-                std = tail.tile([P, groups], F32)
-                nc.scalar.activation(
-                    out=std[:], in_=spread2[:], func=ACT.Sqrt, scale=1.0 / EMB, bias=eps[:, 0:1]
-                )
                 rstd = tail.tile([P, groups], F32)
-                nc.vector.reciprocal(out=rstd[:], in_=std[:])
+                nc.scalar.activation(
+                    out=rstd[:],
+                    in_=spread2[:],
+                    func=ACT.Abs_reciprocal_sqrt,
+                    scale=1.0 / EMB,
+                    bias=eps[:, 0:1],
+                )
                 nc.vector.tensor_tensor(
                     out=centred[:],
                     in0=centred[:],
@@ -298,11 +305,11 @@ def tile_eulerinteractionlayer_pa_kernel(
                 )
                 by_tile = centred[:].rearrange("b (m g) d -> b m g d", m=M_TILES)
                 full = [P, M_TILES, ROUND_FIELDS, EMB]
-                nc.vector.tensor_tensor(
+                nc.gpsimd.tensor_tensor(
                     out=by_tile, in0=by_tile, in1=ln_gain[:].unsqueeze(2).to_broadcast(full), op=ALU.mult
                 )
                 y = tail.tile([P, M_TILES, ROUND_FIELDS, EMB], F32)
-                nc.vector.tensor_tensor(
+                nc.gpsimd.tensor_tensor(
                     out=y[:], in0=by_tile, in1=ln_bias[:].unsqueeze(2).to_broadcast(full), op=ALU.add
                 )
                 for dest, first in ((out_0, 0), (out_1, B_TILES)):

@@ -313,7 +313,7 @@ def tile_eulerinteractionlayer_pa_kernel(
                     out=y[:], in0=by_tile, in1=ln_bias[:].unsqueeze(2).to_broadcast(full), op=ALU.add
                 )
                 for dest, first in ((out_0, 0), (out_1, B_TILES)):
-                    nc.gpsimd.dma_start(
+                    nc.sync.dma_start(
                         out=dest.rearrange("(t b) f d -> b t (f d)", t=B_TILES)[:, :, cols],
                         in_=y[:, first : first + B_TILES, :, :].rearrange("b t g d -> b t (g d)"),
                     )

@@ -27,8 +27,11 @@ ROUND_COLS = ROUND_FIELDS * EMB
 ROUNDS = FIELDS // ROUND_FIELDS
 WIDE = 256
 QUAD = 4
+ROUND_BLOCKS = ROUND_COLS // P
+POLAR_PIECES = 2
 LN_EPS = 1e-5
 ROUNDS_AHEAD = 4
+LOADS_AHEAD = 8
 VECTOR_ROUNDS = 3
 ROUND_MAGIC = 12582912.0
 
@@ -56,7 +59,7 @@ def tile_eulerinteractionlayer_pa_kernel(
     nc = tc.nc
     with (
         tc.tile_pool(name="keep", bufs=1) as keep,
-        tc.tile_pool(name="w_raw", bufs=8) as w_raw_pool,
+        tc.tile_pool(name="w_raw", bufs=LOADS_AHEAD) as w_raw_pool,
         tc.tile_pool(name="w_grouped", bufs=PASSES) as w_grouped_pool,
         tc.tile_pool(name="w_mx", bufs=ROUNDS_AHEAD * PASSES) as w_mx_pool,
         tc.psum_pool(name="acc", bufs=M_TILES) as acc_pool,
@@ -75,10 +78,135 @@ def tile_eulerinteractionlayer_pa_kernel(
         a_scales = keep.tile([P, M_TILES, PASSES, P], U8, align_bytes=64)
         neg_polar = keep.tile([P, M_TILES, K], F32)
         imb_all = keep.tile([P, K], BF16)
-        ln_gain = keep.tile([P, M_TILES, EMB], F32)
-        ln_bias = keep.tile([P, M_TILES, EMB], F32)
+        gain_col = keep.tile([P, ROUND_BLOCKS, 2], F32)
+        bias_col = keep.tile([P, ROUND_BLOCKS, 2], F32)
+
+        w_raw_tiles = {}
+
+        def load_chunk(chunk):
+            rnd, c = divmod(chunk, PASSES)
+            cols = slice(rnd * ROUND_COLS, (rnd + 1) * ROUND_COLS)
+            w_raw = w_raw_pool.tile([P, 4, ROUND_COLS], BF16)
+            for u in range(2):
+                first = c * K_PASS + u * HALF
+                nc.sync.dma_start(
+                    out=w_raw[:, 2 * u : 2 * u + 2, :],
+                    in_=im_w[first : first + HALF, cols].rearrange("(q e) n -> q e n", e=2),
+                )
+            w_raw_tiles[chunk] = w_raw
+
+        def quantise_chunk(chunk):
+            w_raw = w_raw_tiles.pop(chunk)
+            w_grouped = w_grouped_pool.tile([P, ROUND_COLS, 4], BF16, align_bytes=64)
+            regroup = nc.vector.tensor_copy if chunk < VECTOR_ROUNDS * PASSES else nc.scalar.copy
+            regroup(
+                out=w_grouped[:].rearrange("q (n i) t -> q n t i", i=4),
+                in_=w_raw[:].rearrange("q t (n i) -> q n t i", i=4),
+            )
+            codes = w_mx_pool.tile([P, ROUND_COLS], U32, align_bytes=64)
+            scales = w_mx_pool.tile([P, ROUND_COLS], U8, align_bytes=64)
+            for lo, hi in ((0, WIDE), (WIDE, ROUND_COLS)):
+                nc.vector.quantize_mx(
+                    out=codes[:, lo:hi].bitcast(FP8X4),
+                    scales=scales[:, lo:hi],
+                    in_=w_grouped[:, lo:hi, :].rearrange("q n t -> q (n t)"),
+                )
+            return codes, scales
 
         with tc.tile_pool(name="head", bufs=1) as head:
+            bias_rows = head.tile([P, 2, K], BF16)
+            nc.gpsimd.memset(bias_rows[:], 0.0)
+            polar_inputs = ((theta, bias_theta), (log_lam, bias_lam))
+            raws = {}
+            for kind, (x, bias) in enumerate(polar_inputs):
+                nc.sync.dma_start(
+                    out=bias_rows[0:1, kind, :], in_=bias.rearrange("o d g -> o (d g)")
+                )
+                for bt in range(B_TILES):
+                    raw = head.tile([P, K], BF16, tag="raw", bufs=3)
+                    nc.sync.dma_start(
+                        out=raw[:],
+                        in_=x.rearrange("b f d -> b (f d)")[bt * P : (bt + 1) * P, :],
+                    )
+                    raws[kind, bt] = raw
+            for chunk in range(LOADS_AHEAD):
+                load_chunk(chunk)
+
+            for kind in range(2):
+                for bt in range(B_TILES):
+                    by_word = head.tile([P, EMB // 2, FIELDS], F32)
+                    words = raws[kind, bt][:].bitcast(F32).rearrange("b (f w) -> b w f", w=EMB // 2)
+                    x_t = head.tile([P, EMB // 2, P, 2], BF16, bufs=2)
+                    x_t_words = x_t[:].bitcast(F32)
+                    for w0 in range(0, EMB // 2, QUAD):
+                        nc.vector.tensor_copy(
+                            out=by_word[:, w0 : w0 + QUAD, :], in_=words[:, w0 : w0 + QUAD, :]
+                        )
+                        flipped = aux_pool.tile([P, QUAD, P], F32, tag="aux")
+                        for i in range(QUAD):
+                            nc.tensor.transpose(flipped[:, i, :], by_word[:, w0 + i, :], ident_f32[:])
+                        nc.scalar.copy(out=x_t_words[:, w0 : w0 + QUAD, :, 0], in_=flipped[:])
+                    for d0 in range(0, EMB, QUAD):
+                        mixed = aux_pool.tile([P, QUAD, FIELDS], F32, tag="aux")
+                        for i in range(QUAD):
+                            d = d0 + i
+                            nc.tensor.matmul(
+                                mixed[:, i, :],
+                                lhsT=ones_bf[:],
+                                rhs=bias_rows[:, kind, d * FIELDS : (d + 1) * FIELDS],
+                                start=True,
+                                stop=False,
+                            )
+                            nc.tensor.matmul(
+                                mixed[:, i, :],
+                                lhsT=x_t[:, d // 2, :, d % 2],
+                                rhs=orders[:],
+                                start=False,
+                                stop=True,
+                            )
+                        by_field = mixed[:].rearrange("b i g -> b g i")
+                        if kind == 0:
+                            nc.scalar.activation(
+                                out=neg_polar[:, B_TILES + bt, :].rearrange(
+                                    "b (g d) -> b g d", d=EMB
+                                )[:, :, d0 : d0 + QUAD],
+                                in_=by_field,
+                                func=ACT.Copy,
+                                scale=1.0 / (2.0 * math.pi),
+                            )
+                        else:
+                            nc.scalar.activation(
+                                out=neg_polar[:, bt, :].rearrange("b (g d) -> b g d", d=EMB)[
+                                    :, :, d0 : d0 + QUAD
+                                ],
+                                in_=by_field,
+                                func=ACT.Exp,
+                            )
+            for bt in range(B_TILES):
+                for piece in range(POLAR_PIECES):
+                    span = slice(piece * K // POLAR_PIECES, (piece + 1) * K // POLAR_PIECES)
+                    lam = neg_polar[:, bt, span]
+                    turns = neg_polar[:, B_TILES + bt, span]
+                    part = head.tile([P, K // POLAR_PIECES], F32, bufs=3)
+                    nc.vector.tensor_scalar(
+                        out=part[:],
+                        in0=turns,
+                        scalar1=ROUND_MAGIC,
+                        scalar2=ROUND_MAGIC,
+                        op0=ALU.add,
+                        op1=ALU.subtract,
+                    )
+                    nc.vector.tensor_tensor(out=part[:], in0=part[:], in1=turns, op=ALU.subtract)
+                    nc.scalar.activation(out=turns, in_=part[:], func=ACT.Sin, scale=2.0 * math.pi)
+                    nc.scalar.activation(out=part[:], in_=part[:], func=ACT.Sin, scale=math.pi)
+                    nc.scalar.activation(
+                        out=part[:], in_=part[:], func=ACT.Square, scale=math.sqrt(2.0)
+                    )
+                    nc.vector.tensor_tensor(out=turns, in0=turns, in1=lam, op=ALU.mult)
+                    nc.vector.scalar_tensor_tensor(
+                        out=lam, in0=part[:], scalar=1.0, in1=lam, op0=ALU.subtract, op1=ALU.mult
+                    )
+
             for m in range(M_TILES):
                 source = r if m < B_TILES else p
                 rows = slice((m % B_TILES) * P, (m % B_TILES + 1) * P)
@@ -95,7 +223,7 @@ def tile_eulerinteractionlayer_pa_kernel(
                             nc.tensor.transpose(
                                 flipped[:, j, u, :], raw_words[:, first : first + P], ident_f32[:]
                             )
-                    nc.scalar.copy(
+                    nc.vector.tensor_copy(
                         out=a_grouped_words[:, c0 : c0 + 2, :, :],
                         in_=flipped[:].rearrange("q j u b -> q j b u"),
                     )
@@ -107,109 +235,27 @@ def tile_eulerinteractionlayer_pa_kernel(
                     )
 
             nc.sync.dma_start(out=imb_all[:], in_=im_b.partition_broadcast(P))
-            for vec, dest, first in (
-                (norm_r_w, ln_gain, 0),
-                (norm_p_w, ln_gain, B_TILES),
-                (norm_r_b, ln_bias, 0),
-                (norm_p_b, ln_bias, B_TILES),
+            for vec, dest, t in (
+                (norm_r_w, gain_col, 0),
+                (norm_p_w, gain_col, 1),
+                (norm_r_b, bias_col, 0),
+                (norm_p_b, bias_col, 1),
             ):
-                spread = head.tile([P, EMB], BF16, tag="spread", bufs=4)
+                spread = head.tile([P, EMB], BF16, bufs=4)
                 nc.sync.dma_start(out=spread[:], in_=vec.partition_broadcast(P))
+                equal_rows = head.tile([P, ROUND_FIELDS, EMB], F32)
                 nc.vector.tensor_copy(
-                    out=dest[:, first : first + B_TILES, :],
-                    in_=spread[:].unsqueeze(1).to_broadcast([P, B_TILES, EMB]),
+                    out=equal_rows[:],
+                    in_=spread[:].unsqueeze(1).to_broadcast([P, ROUND_FIELDS, EMB]),
                 )
-
-            for kind, x, bias in (("theta", theta, bias_theta), ("lam", log_lam, bias_lam)):
-                bias_row = head.tile([P, K], BF16, tag="bias_row", bufs=1)
-                nc.gpsimd.memset(bias_row[:], 0.0)
-                nc.sync.dma_start(out=bias_row[0:1, :], in_=bias.rearrange("o d g -> o (d g)"))
-                for bt in range(B_TILES):
-                    raw = head.tile([P, K], BF16, tag="raw", bufs=3)
-                    nc.sync.dma_start(
-                        out=raw[:],
-                        in_=x.rearrange("b f d -> b (f d)")[bt * P : (bt + 1) * P, :],
+                flipped = aux_pool.tile([P, ROUND_BLOCKS, P], F32, tag="aux")
+                for block in range(ROUND_BLOCKS):
+                    nc.tensor.transpose(
+                        flipped[:, block, :],
+                        equal_rows[:].rearrange("b g d -> b (g d)")[:, block * P : (block + 1) * P],
+                        ident_f32[:],
                     )
-                    by_word = head.tile([P, EMB // 2, FIELDS], F32, tag="by_word", bufs=1)
-                    nc.vector.tensor_copy(
-                        out=by_word[:],
-                        in_=raw[:].bitcast(F32).rearrange("b (f w) -> b w f", w=EMB // 2),
-                    )
-                    x_t = head.tile([P, EMB // 2, P, 2], BF16, tag="x_t", bufs=2)
-                    x_t_words = x_t[:].bitcast(F32)
-                    for w0 in range(0, EMB // 2, QUAD):
-                        flipped = aux_pool.tile([P, QUAD, P], F32, tag="aux")
-                        for i in range(QUAD):
-                            nc.tensor.transpose(flipped[:, i, :], by_word[:, w0 + i, :], ident_f32[:])
-                        nc.scalar.copy(
-                            out=x_t_words[:, w0 : w0 + QUAD, :, 0], in_=flipped[:]
-                        )
-                    for d0 in range(0, EMB, QUAD):
-                        mixed = aux_pool.tile([P, QUAD, FIELDS], F32, tag="aux")
-                        for i in range(QUAD):
-                            d = d0 + i
-                            nc.tensor.matmul(
-                                mixed[:, i, :],
-                                lhsT=ones_bf[:],
-                                rhs=bias_row[:, d * FIELDS : (d + 1) * FIELDS],
-                                start=True,
-                                stop=False,
-                            )
-                            nc.tensor.matmul(
-                                mixed[:, i, :],
-                                lhsT=x_t[:, d // 2, :, d % 2],
-                                rhs=orders[:],
-                                start=False,
-                                stop=True,
-                            )
-                        by_field = mixed[:].rearrange("b i g -> b g i")
-                        if kind == "lam":
-                            nc.scalar.activation(
-                                out=neg_polar[:, bt, :].rearrange("b (g d) -> b g d", d=EMB)[
-                                    :, :, d0 : d0 + QUAD
-                                ],
-                                in_=by_field,
-                                func=ACT.Exp,
-                            )
-                        else:
-                            nc.scalar.activation(
-                                out=neg_polar[:, B_TILES + bt, :].rearrange(
-                                    "b (g d) -> b g d", d=EMB
-                                )[:, :, d0 : d0 + QUAD],
-                                in_=by_field,
-                                func=ACT.Copy,
-                                scale=1.0 / (2.0 * math.pi),
-                            )
-            for bt in range(B_TILES):
-                lam = neg_polar[:, bt, :]
-                turns = neg_polar[:, B_TILES + bt, :]
-                part = head.tile([P, K], F32, bufs=2)
-                nc.vector.tensor_scalar(
-                    out=part[:],
-                    in0=turns,
-                    scalar1=ROUND_MAGIC,
-                    scalar2=ROUND_MAGIC,
-                    op0=ALU.add,
-                    op1=ALU.subtract,
-                )
-                nc.vector.tensor_tensor(out=part[:], in0=part[:], in1=turns, op=ALU.subtract)
-                nc.scalar.activation(
-                    out=neg_polar[:, B_TILES + bt, :], in_=part[:], func=ACT.Sin, scale=2.0 * math.pi
-                )
-                half_sin = part
-                nc.scalar.activation(out=half_sin[:], in_=part[:], func=ACT.Sin, scale=math.pi)
-                nc.scalar.activation(
-                    out=half_sin[:], in_=half_sin[:], func=ACT.Square, scale=math.sqrt(2.0)
-                )
-                nc.vector.tensor_tensor(
-                    out=neg_polar[:, B_TILES + bt, :],
-                    in0=neg_polar[:, B_TILES + bt, :],
-                    in1=lam,
-                    op=ALU.mult,
-                )
-                nc.vector.scalar_tensor_tensor(
-                    out=lam, in0=half_sin[:], scalar=1.0, in1=lam, op0=ALU.subtract, op1=ALU.mult
-                )
+                nc.vector.tensor_copy(out=dest[:, :, t], in_=flipped[:, :, 0])
 
         with tc.tile_pool(name="tail", bufs=2) as tail:
             for rnd in range(ROUNDS):
@@ -217,34 +263,12 @@ def tile_eulerinteractionlayer_pa_kernel(
                 w_codes = []
                 w_scales = []
                 for c in range(PASSES):
-                    w_raw = w_raw_pool.tile([P, 4, ROUND_COLS], BF16)
-                    for u in range(2):
-                        first = c * K_PASS + u * HALF
-                        nc.sync.dma_start(
-                            out=w_raw[:, 2 * u : 2 * u + 2, :],
-                            in_=im_w[first : first + HALF, cols].rearrange("(q e) n -> q e n", e=2),
-                        )
-                    w_grouped = w_grouped_pool.tile([P, ROUND_COLS, 4], BF16, align_bytes=64)
-                    if rnd < VECTOR_ROUNDS:
-                        nc.vector.tensor_copy(
-                            out=w_grouped[:].rearrange("q (n i) t -> q n t i", i=4),
-                            in_=w_raw[:].rearrange("q t (n i) -> q n t i", i=4),
-                        )
-                    else:
-                        nc.scalar.copy(
-                            out=w_grouped[:].rearrange("q (n i) t -> q n t i", i=4),
-                            in_=w_raw[:].rearrange("q t (n i) -> q n t i", i=4),
-                        )
-                    codes = w_mx_pool.tile([P, ROUND_COLS], U32, align_bytes=64, name="codes")
-                    scales = w_mx_pool.tile([P, ROUND_COLS], U8, align_bytes=64, name="scales")
-                    for lo, hi in ((0, WIDE), (WIDE, ROUND_COLS)):
-                        nc.vector.quantize_mx(
-                            out=codes[:, lo:hi].bitcast(FP8X4),
-                            scales=scales[:, lo:hi],
-                            in_=w_grouped[:, lo:hi, :].rearrange("q n t -> q (n t)"),
-                        )
+                    chunk = rnd * PASSES + c
+                    codes, scales = quantise_chunk(chunk)
                     w_codes.append(codes)
                     w_scales.append(scales)
+                    if chunk + LOADS_AHEAD < ROUNDS * PASSES:
+                        load_chunk(chunk + LOADS_AHEAD)
 
                 biased = tail.tile([P, M_TILES, ROUND_COLS], F32)
                 for m in range(M_TILES):
@@ -303,17 +327,34 @@ def tile_eulerinteractionlayer_pa_kernel(
                     in1=rstd[:].unsqueeze(2).to_broadcast([P, groups, EMB]),
                     op=ALU.mult,
                 )
-                by_tile = centred[:].rearrange("b (m g) d -> b m g d", m=M_TILES)
-                full = [P, M_TILES, ROUND_FIELDS, EMB]
-                nc.gpsimd.tensor_tensor(
-                    out=by_tile, in0=by_tile, in1=ln_gain[:].unsqueeze(2).to_broadcast(full), op=ALU.mult
-                )
-                y = tail.tile([P, M_TILES, ROUND_FIELDS, EMB], F32)
-                nc.gpsimd.tensor_tensor(
-                    out=y[:], in0=by_tile, in1=ln_bias[:].unsqueeze(2).to_broadcast(full), op=ALU.add
-                )
+                normed = centred[:].rearrange("b (m g) d -> b m (g d)", m=M_TILES)
+                y_t = tail.tile([P, ROUND_BLOCKS, M_TILES, P], F32)
+                for block in range(ROUND_BLOCKS):
+                    flipped = aux_pool.tile([P, M_TILES, P], F32, tag="aux")
+                    for m in range(M_TILES):
+                        nc.tensor.transpose(
+                            flipped[:, m, :], normed[:, m, block * P : (block + 1) * P], ident_f32[:]
+                        )
+                    for t in range(2):
+                        tiles = slice(t * B_TILES, (t + 1) * B_TILES)
+                        nc.scalar.activation(
+                            out=y_t[:, block, tiles, :],
+                            in_=flipped[:, tiles, :],
+                            func=ACT.Identity,
+                            scale=gain_col[:, block, t : t + 1],
+                            bias=bias_col[:, block, t : t + 1],
+                        )
+                y = tail.tile([P, M_TILES * ROUND_BLOCKS, P], F32)
+                for j0 in range(0, M_TILES * ROUND_BLOCKS, QUAD):
+                    back = aux_pool.tile([P, QUAD, P], F32, tag="aux")
+                    for i in range(QUAD):
+                        m, block = divmod(j0 + i, ROUND_BLOCKS)
+                        nc.tensor.transpose(back[:, i, :], y_t[:, block, m, :], ident_f32[:])
+                    nc.scalar.copy(out=y[:, j0 : j0 + QUAD, :], in_=back[:])
                 for dest, first in ((out_0, 0), (out_1, B_TILES)):
                     nc.sync.dma_start(
                         out=dest.rearrange("(t b) f d -> b t (f d)", t=B_TILES)[:, :, cols],
-                        in_=y[:, first : first + B_TILES, :, :].rearrange("b t g d -> b t (g d)"),
+                        in_=y[:].rearrange("b (m k) n -> b m (k n)", m=M_TILES)[
+                            :, first : first + B_TILES, :
+                        ],
                     )

import math

import concourse.mybir as mybir
from concourse.masks import make_identity

F32 = mybir.dt.float32
BF16 = mybir.dt.bfloat16
U32 = mybir.dt.uint32
U8 = mybir.dt.uint8
FP8X4 = mybir.dt.float8_e4m3fn_x4
ACT = mybir.ActivationFunctionType
ALU = mybir.AluOpType
AXIS_X = mybir.AxisListType.X

P = 128
BATCH = 256
FIELDS = 128
EMB = 24
K = FIELDS * EMB
B_TILES = BATCH // P
M_TILES = 2 * B_TILES
K_PASS = 512
PASSES = K // K_PASS
HALF = K_PASS // 2
ROUND_FIELDS = 16
ROUND_COLS = ROUND_FIELDS * EMB
ROUNDS = FIELDS // ROUND_FIELDS
WIDE = 256
QUAD = 4
ROUND_BLOCKS = ROUND_COLS // P
POLAR_PIECES = 2
LN_EPS = 1e-5
ROUNDS_AHEAD = 4
LOADS_AHEAD = 8
VECTOR_ROUNDS = 3
ROUND_MAGIC = 12582912.0

FLOPS = 2 * (2 * BATCH) * K * K + 2 * 2 * BATCH * EMB * FIELDS * FIELDS


def tile_eulerinteractionlayer_pa_kernel(
    tc,
    r,
    p,
    log_lam,
    theta,
    inter_orders,
    im_w,
    im_b,
    bias_lam,
    bias_theta,
    norm_r_w,
    norm_r_b,
    norm_p_w,
    norm_p_b,
    out_0,
    out_1,
):
    nc = tc.nc
    with (
        tc.tile_pool(name="keep", bufs=1) as keep,
        tc.tile_pool(name="w_raw", bufs=LOADS_AHEAD) as w_raw_pool,
        tc.tile_pool(name="w_grouped", bufs=PASSES) as w_grouped_pool,
        tc.tile_pool(name="w_mx", bufs=ROUNDS_AHEAD * PASSES) as w_mx_pool,
        tc.psum_pool(name="acc", bufs=M_TILES) as acc_pool,
        tc.psum_pool(name="aux", bufs=4) as aux_pool,
    ):
        ident_f32 = keep.tile([P, P], F32)
        make_identity(nc, ident_f32[:])
        ones_bf = keep.tile([P, P], BF16)
        nc.vector.memset(ones_bf[:], 1.0)
        eps = keep.tile([P, 1], F32)
        nc.vector.memset(eps[:], LN_EPS)
        orders = keep.tile([P, FIELDS], BF16)
        nc.sync.dma_start(out=orders[:], in_=inter_orders)

        a_codes = keep.tile([P, M_TILES, PASSES, P], U32, align_bytes=64)
        a_scales = keep.tile([P, M_TILES, PASSES, P], U8, align_bytes=64)
        neg_polar = keep.tile([P, M_TILES, K], F32)
        imb_all = keep.tile([P, K], BF16)
        gain_col = keep.tile([P, ROUND_BLOCKS, 2], F32)
        bias_col = keep.tile([P, ROUND_BLOCKS, 2], F32)

        w_raw_tiles = {}

        def load_chunk(chunk):
            rnd, c = divmod(chunk, PASSES)
            cols = slice(rnd * ROUND_COLS, (rnd + 1) * ROUND_COLS)
            w_raw = w_raw_pool.tile([P, 4, ROUND_COLS], BF16)
            for u in range(2):
                first = c * K_PASS + u * HALF
                nc.sync.dma_start(
                    out=w_raw[:, 2 * u : 2 * u + 2, :],
                    in_=im_w[first : first + HALF, cols].rearrange("(q e) n -> q e n", e=2),
                )
            w_raw_tiles[chunk] = w_raw

        def quantise_chunk(chunk):
            w_raw = w_raw_tiles.pop(chunk)
            w_grouped = w_grouped_pool.tile([P, ROUND_COLS, 4], BF16, align_bytes=64)
            regroup = nc.vector.tensor_copy if chunk < VECTOR_ROUNDS * PASSES else nc.scalar.copy
            regroup(
                out=w_grouped[:].rearrange("q (n i) t -> q n t i", i=4),
                in_=w_raw[:].rearrange("q t (n i) -> q n t i", i=4),
            )
            codes = w_mx_pool.tile([P, ROUND_COLS], U32, align_bytes=64)
            scales = w_mx_pool.tile([P, ROUND_COLS], U8, align_bytes=64)
            for lo, hi in ((0, WIDE), (WIDE, ROUND_COLS)):
                nc.vector.quantize_mx(
                    out=codes[:, lo:hi].bitcast(FP8X4),
                    scales=scales[:, lo:hi],
                    in_=w_grouped[:, lo:hi, :].rearrange("q n t -> q (n t)"),
                )
            return codes, scales

        with tc.tile_pool(name="head", bufs=1) as head:
            bias_rows = head.tile([P, 2, K], BF16)
            nc.gpsimd.memset(bias_rows[:], 0.0)
            polar_inputs = ((theta, bias_theta), (log_lam, bias_lam))
            raws = {}
            for kind, (x, bias) in enumerate(polar_inputs):
                nc.sync.dma_start(
                    out=bias_rows[0:1, kind, :], in_=bias.rearrange("o d g -> o (d g)")
                )
                for bt in range(B_TILES):
                    raw = head.tile([P, K], BF16, tag="raw", bufs=3)
                    nc.sync.dma_start(
                        out=raw[:],
                        in_=x.rearrange("b f d -> b (f d)")[bt * P : (bt + 1) * P, :],
                    )
                    raws[kind, bt] = raw
            for chunk in range(LOADS_AHEAD):
                load_chunk(chunk)

            for kind in range(2):
                for bt in range(B_TILES):
                    by_word = head.tile([P, EMB // 2, FIELDS], F32)
                    words = raws[kind, bt][:].bitcast(F32).rearrange("b (f w) -> b w f", w=EMB // 2)
                    x_t = head.tile([P, EMB // 2, P, 2], BF16, bufs=2)
                    x_t_words = x_t[:].bitcast(F32)
                    for w0 in range(0, EMB // 2, QUAD):
                        nc.vector.tensor_copy(
                            out=by_word[:, w0 : w0 + QUAD, :], in_=words[:, w0 : w0 + QUAD, :]
                        )
                        flipped = aux_pool.tile([P, QUAD, P], F32, tag="aux")
                        for i in range(QUAD):
                            nc.tensor.transpose(flipped[:, i, :], by_word[:, w0 + i, :], ident_f32[:])
                        nc.scalar.copy(out=x_t_words[:, w0 : w0 + QUAD, :, 0], in_=flipped[:])
                    for d0 in range(0, EMB, QUAD):
                        mixed = aux_pool.tile([P, QUAD, FIELDS], F32, tag="aux")
                        for i in range(QUAD):
                            d = d0 + i
                            nc.tensor.matmul(
                                mixed[:, i, :],
                                lhsT=ones_bf[:],
                                rhs=bias_rows[:, kind, d * FIELDS : (d + 1) * FIELDS],
                                start=True,
                                stop=False,
                            )
                            nc.tensor.matmul(
                                mixed[:, i, :],
                                lhsT=x_t[:, d // 2, :, d % 2],
                                rhs=orders[:],
                                start=False,
                                stop=True,
                            )
                        by_field = mixed[:].rearrange("b i g -> b g i")
                        if kind == 0:
                            nc.scalar.activation(
                                out=neg_polar[:, B_TILES + bt, :].rearrange(
                                    "b (g d) -> b g d", d=EMB
                                )[:, :, d0 : d0 + QUAD],
                                in_=by_field,
                                func=ACT.Copy,
                                scale=1.0 / (2.0 * math.pi),
                            )
                        else:
                            nc.scalar.activation(
                                out=neg_polar[:, bt, :].rearrange("b (g d) -> b g d", d=EMB)[
                                    :, :, d0 : d0 + QUAD
                                ],
                                in_=by_field,
                                func=ACT.Exp,
                            )
            for bt in range(B_TILES):
                for piece in range(POLAR_PIECES):
                    span = slice(piece * K // POLAR_PIECES, (piece + 1) * K // POLAR_PIECES)
                    lam = neg_polar[:, bt, span]
                    turns = neg_polar[:, B_TILES + bt, span]
                    part = head.tile([P, K // POLAR_PIECES], F32, bufs=3)
                    nc.vector.tensor_scalar(
                        out=part[:],
                        in0=turns,
                        scalar1=ROUND_MAGIC,
                        scalar2=ROUND_MAGIC,
                        op0=ALU.add,
                        op1=ALU.subtract,
                    )
                    nc.vector.tensor_tensor(out=part[:], in0=part[:], in1=turns, op=ALU.subtract)
                    nc.scalar.activation(out=turns, in_=part[:], func=ACT.Sin, scale=2.0 * math.pi)
                    nc.scalar.activation(out=part[:], in_=part[:], func=ACT.Sin, scale=math.pi)
                    nc.scalar.activation(
                        out=part[:], in_=part[:], func=ACT.Square, scale=math.sqrt(2.0)
                    )
                    nc.vector.tensor_tensor(out=turns, in0=turns, in1=lam, op=ALU.mult)
                    nc.vector.scalar_tensor_tensor(
                        out=lam, in0=part[:], scalar=1.0, in1=lam, op0=ALU.subtract, op1=ALU.mult
                    )

            for m in range(M_TILES):
                source = r if m < B_TILES else p
                rows = slice((m % B_TILES) * P, (m % B_TILES + 1) * P)
                raw = head.tile([P, K], BF16, tag="raw", bufs=3)
                nc.sync.dma_start(out=raw[:], in_=source.rearrange("b f d -> b (f d)")[rows, :])
                raw_words = raw[:].bitcast(F32)
                a_grouped = head.tile([P, PASSES, P, 4], BF16, align_bytes=64)
                a_grouped_words = a_grouped[:].bitcast(F32)
                for c0 in range(0, PASSES, 2):
                    flipped = aux_pool.tile([P, 2, 2, P], F32, tag="aux")
                    for j in range(2):
                        for u in range(2):
                            first = ((c0 + j) * K_PASS + u * HALF) // 2
                            nc.tensor.transpose(
                                flipped[:, j, u, :], raw_words[:, first : first + P], ident_f32[:]
                            )
                    nc.vector.tensor_copy(
                        out=a_grouped_words[:, c0 : c0 + 2, :, :],
                        in_=flipped[:].rearrange("q j u b -> q j b u"),
                    )
                for lo, hi in ((0, 4), (4, 6)):
                    nc.vector.quantize_mx(
                        out=a_codes[:, m, lo:hi, :].rearrange("q c b -> q (c b)").bitcast(FP8X4),
                        scales=a_scales[:, m, lo:hi, :].rearrange("q c b -> q (c b)"),
                        in_=a_grouped[:, lo:hi, :, :].rearrange("q c b t -> q (c b t)"),
                    )

            nc.sync.dma_start(out=imb_all[:], in_=im_b.partition_broadcast(P))
            for vec, dest, t in (
                (norm_r_w, gain_col, 0),
                (norm_p_w, gain_col, 1),
                (norm_r_b, bias_col, 0),
                (norm_p_b, bias_col, 1),
            ):
                spread = head.tile([P, EMB], BF16, bufs=4)
                nc.sync.dma_start(out=spread[:], in_=vec.partition_broadcast(P))
                equal_rows = head.tile([P, ROUND_FIELDS, EMB], F32)
                nc.vector.tensor_copy(
                    out=equal_rows[:],
                    in_=spread[:].unsqueeze(1).to_broadcast([P, ROUND_FIELDS, EMB]),
                )
                flipped = aux_pool.tile([P, ROUND_BLOCKS, P], F32, tag="aux")
                for block in range(ROUND_BLOCKS):
                    nc.tensor.transpose(
                        flipped[:, block, :],
                        equal_rows[:].rearrange("b g d -> b (g d)")[:, block * P : (block + 1) * P],
                        ident_f32[:],
                    )
                nc.vector.tensor_copy(out=dest[:, :, t], in_=flipped[:, :, 0])

        with tc.tile_pool(name="tail", bufs=2) as tail:
            for rnd in range(ROUNDS):
                cols = slice(rnd * ROUND_COLS, (rnd + 1) * ROUND_COLS)
                w_codes = []
                w_scales = []
                for c in range(PASSES):
                    chunk = rnd * PASSES + c
                    codes, scales = quantise_chunk(chunk)
                    w_codes.append(codes)
                    w_scales.append(scales)
                    if chunk + LOADS_AHEAD < ROUNDS * PASSES:
                        load_chunk(chunk + LOADS_AHEAD)

                biased = tail.tile([P, M_TILES, ROUND_COLS], F32)
                for m in range(M_TILES):
                    acc = acc_pool.tile([P, ROUND_COLS], F32)
                    for lo, hi in ((0, WIDE), (WIDE, ROUND_COLS)):
                        for c in range(PASSES):
                            nc.tensor.matmul_mx(
                                out=acc[:, lo:hi],
                                lhsT=a_codes[:, m, c, :].bitcast(FP8X4),
                                lhsT_scale=a_scales[:, m, c, :],
                                rhs=w_codes[c][:, lo:hi].bitcast(FP8X4),
                                rhs_scale=w_scales[c][:, lo:hi],
                                start=(c == 0),
                                stop=(c == PASSES - 1),
                            )
                    nc.vector.tensor_tensor(
                        out=biased[:, m, :], in0=acc[:], in1=imb_all[:, cols], op=ALU.add
                    )
                groups = M_TILES * ROUND_FIELDS
                o = tail.tile([P, M_TILES, ROUND_COLS], F32)
                nc.vector.scalar_tensor_tensor(
                    out=o[:],
                    in0=biased[:],
                    scalar=0.0,
                    in1=neg_polar[:, :, cols],
                    op0=ALU.max,
                    op1=ALU.subtract,
                )
                o_groups = o[:].rearrange("b m (g d) -> b (m g) d", d=EMB)
                total = tail.tile([P, groups], F32)
                nc.vector.tensor_reduce(out=total[:], in_=o_groups, axis=AXIS_X, op=ALU.add)
                centred = tail.tile([P, groups, EMB], F32)
                nc.vector.scalar_tensor_tensor(
                    out=centred[:],
                    in0=total[:].unsqueeze(2).to_broadcast([P, groups, EMB]),
                    scalar=-1.0 / EMB,
                    in1=o_groups,
                    op0=ALU.mult,
                    op1=ALU.add,
                )
                squares = tail.tile([P, groups, EMB], F32)
                nc.scalar.activation(out=squares[:], in_=centred[:], func=ACT.Square)
                spread2 = tail.tile([P, groups], F32)
                nc.vector.tensor_reduce(out=spread2[:], in_=squares[:], axis=AXIS_X, op=ALU.add)
                rstd = tail.tile([P, groups], F32)
                nc.scalar.activation(
                    out=rstd[:],
                    in_=spread2[:],
                    func=ACT.Abs_reciprocal_sqrt,
                    scale=1.0 / EMB,
                    bias=eps[:, 0:1],
                )
                nc.vector.tensor_tensor(
                    out=centred[:],
                    in0=centred[:],
                    in1=rstd[:].unsqueeze(2).to_broadcast([P, groups, EMB]),
                    op=ALU.mult,
                )
                normed = centred[:].rearrange("b (m g) d -> b m (g d)", m=M_TILES)
                y_t = tail.tile([P, ROUND_BLOCKS, M_TILES, P], F32)
                for block in range(ROUND_BLOCKS):
                    flipped = aux_pool.tile([P, M_TILES, P], F32, tag="aux")
                    for m in range(M_TILES):
                        nc.tensor.transpose(
                            flipped[:, m, :], normed[:, m, block * P : (block + 1) * P], ident_f32[:]
                        )
                    for t in range(2):
                        tiles = slice(t * B_TILES, (t + 1) * B_TILES)
                        nc.scalar.activation(
                            out=y_t[:, block, tiles, :],
                            in_=flipped[:, tiles, :],
                            func=ACT.Identity,
                            scale=gain_col[:, block, t : t + 1],
                            bias=bias_col[:, block, t : t + 1],
                        )
                y = tail.tile([P, M_TILES * ROUND_BLOCKS, P], F32)
                for j0 in range(0, M_TILES * ROUND_BLOCKS, QUAD):
                    back = aux_pool.tile([P, QUAD, P], F32, tag="aux")
                    for i in range(QUAD):
                        m, block = divmod(j0 + i, ROUND_BLOCKS)
                        nc.tensor.transpose(back[:, i, :], y_t[:, block, m, :], ident_f32[:])
                    nc.scalar.copy(out=y[:, j0 : j0 + QUAD, :], in_=back[:])
                for dest, first in ((out_0, 0), (out_1, B_TILES)):
                    nc.sync.dma_start(
                        out=dest.rearrange("(t b) f d -> b t (f d)", t=B_TILES)[:, :, cols],
                        in_=y[:].rearrange("b (m k) n -> b m (k n)", m=M_TILES)[
                            :, first : first + B_TILES, :
                        ],
                    )
